import numpy as np
import ml_dtypes


def mxq(x, axis, fmt="e4m3"):
    dtype, down = {"e4m3": (ml_dtypes.float8_e4m3fn, 7), "e5m2": (ml_dtypes.float8_e5m2, 14)}[fmt]
    v = np.moveaxis(np.asarray(x, np.float32).astype(ml_dtypes.bfloat16).astype(np.float64), axis, -1)
    blocks = v.reshape(v.shape[:-1] + (-1, 32))
    amax = np.abs(blocks).max(-1, keepdims=True)
    byte = np.maximum(np.where(amax > 0, np.frexp(amax)[1] - 1 + 127, 0) - down, 1)
    scale = np.exp2(byte - 127.0)
    codes = (blocks / scale).astype(np.float32).astype(dtype).astype(np.float64)
    return np.moveaxis((codes * scale).reshape(v.shape), -1, axis)


WIDE = False


def mx_kscale(k):
    if not WIDE:
        return np.ones(k)
    levels = np.array([10, -10, 5, -5, 0])
    if k % 512:
        return np.exp2(np.random.permutation(np.resize(levels, k // 32))).repeat(32)
    a = np.empty((k // 512, 16))
    for p in range(k // 512):
        a[p, :8] = np.random.permutation(np.resize(levels, 8))
        for g in range(8):
            far = levels[np.abs(levels - a[p, g]) >= 10]
            a[p, g + 8] = far[np.random.randint(len(far))]
    return np.exp2(a.ravel()).repeat(32)


BF16 = ml_dtypes.bfloat16


def bf(x):
    return np.asarray(x, np.float32).astype(BF16)


def f64(x):
    return np.asarray(x).astype(np.float64)


B, N, SIZE, CH = 128, 16, 1024, 256


def sigmoid(v):
    return 1.0 / (1.0 + np.exp(-v))


def setup_inputs():
    s = mx_kscale(SIZE)
    d = {"z0": bf(np.random.standard_normal((B, SIZE)) * s),
         "h_tilde": bf(np.random.standard_normal((B, CH)) * np.sqrt(N)),
         "fc_sum": bf(np.random.standard_normal((B, CH)) * 1.2)}
    for g in ("i", "o", "u"):
        d["W_" + g] = bf(np.random.standard_normal((CH, SIZE)) / np.sqrt(SIZE) / s)
        d["U_" + g] = bf(np.random.standard_normal((CH, CH)) / np.sqrt(CH * N))
        d["b_" + g] = bf(np.random.standard_normal(CH) * 0.5)
    return d


def reference(z0, h_tilde, fc_sum, W_i, U_i, b_i, W_o, U_o, b_o, W_u, U_u, b_u):
    zq = mxq(f64(z0), 1, "e4m3")
    ht = f64(h_tilde)
    i_j = sigmoid((zq @ mxq(f64(W_i), 1, "e4m3").T) + ht @ f64(U_i).T + f64(b_i))
    o_j = sigmoid((zq @ mxq(f64(W_o), 1, "e4m3").T) + ht @ f64(U_o).T + f64(b_o))
    u_j = np.tanh((zq @ mxq(f64(W_u), 1, "e4m3").T) + ht @ f64(U_u).T + f64(b_u))
    c_j = i_j * u_j + f64(fc_sum)
    h_j = o_j * np.tanh(c_j)
    return np.concatenate([h_j, c_j], axis=-1)

@@ -1,0 +1,222 @@
+from contextlib import ExitStack
+
+import concourse.mybir as mybir
+from concourse.masks import make_identity
+
+F32 = mybir.dt.float32
+BF16 = mybir.dt.bfloat16
+U32 = mybir.dt.uint32
+U8 = mybir.dt.uint8
+FP8X4 = mybir.dt.float8_e4m3fn_x4
+ACT = mybir.ActivationFunctionType
+ALU = mybir.AluOpType
+
+P = 128
+SIZE = 1024
+CH = 256
+GATES = 3
+ROW_BLOCKS = CH // P
+PASSES = SIZE // (4 * P)
+HALVES = 2
+WORDS = PASSES * P
+BANK_SLOTS = 4
+
+FLOPS = 2 * P * GATES * CH * (SIZE + CH)
+
+
+def word_blocks(rows):
+    words = rows.bitcast(F32)
+    return [words[:, s * P : (s + 1) * P] for s in range(words.shape[1] // P)]
+
+
+def alternate_blocks(rows):
+    words = rows.bitcast(F32)
+    return [
+        words[:, 2 * P * g + half : 2 * P * (g + 1) : 2]
+        for g in range(PASSES)
+        for half in range(HALVES)
+    ]
+
+
+def transpose_words(nc, banks, blocks, ident):
+    bank = banks.tile([P, BANK_SLOTS, P], F32, tag="bank", name="bank")
+    for slot in range(len(blocks)):
+        nc.tensor.transpose(out=bank[:, slot, :], in_=blocks[slot], identity=ident[:])
+    return bank
+
+
+def pack_rows(nc, stage, bank, codes, scales):
+    grouped = stage.tile([P, SIZE], BF16, align_bytes=64, name="grouped")
+    nc.scalar.copy(
+        out=grouped[:].bitcast(F32).rearrange("p (g r u) -> p g r u", g=PASSES, u=HALVES),
+        in_=bank[:].rearrange("p (g u) r -> p g r u", u=HALVES),
+    )
+    nc.vector.quantize_mx(out=codes.bitcast(FP8X4), scales=scales, in_=grouped[:])
+
+
+def by_parity(pairs, e):
+    return pairs[:].bitcast(BF16).rearrange("p (c e) -> p c e", e=2)[:, :, e]
+
+
+def from_blocks(sums_ps):
+    return sums_ps.rearrange("p (b r) -> p r b", b=ROW_BLOCKS)
+
+
+def channels(ap):
+    return ap.rearrange("p (r b) -> p r b", b=ROW_BLOCKS)
+
+
+def tile_treelstm_pb_s_kernel(
+    tc, z0, h_tilde, fc_sum, W_i, U_i, b_i, W_o, U_o, b_o, W_u, U_u, b_u, out
+):
+    nc = tc.nc
+    w_dram = (W_i, W_u, W_o)
+    u_dram = (U_i, U_u, U_o)
+    b_dram = (b_i, b_u, b_o)
+    gate_func = (ACT.Sigmoid, ACT.Tanh, ACT.Sigmoid)
+
+    with ExitStack() as ctx:
+        keep = ctx.enter_context(tc.tile_pool(name="keep", bufs=1))
+        stage = ctx.enter_context(tc.tile_pool(name="stage", bufs=4))
+        banks = ctx.enter_context(tc.psum_pool(name="banks", bufs=5))
+        sums = ctx.enter_context(tc.psum_pool(name="sums", bufs=GATES))
+        ctx.enter_context(tc.manual_schedule())
+
+        bias_rows = keep.tile([P, CH], BF16, name="bias_rows")
+        nc.vector.memset(bias_rows[:], 0.0)
+        ident = keep.tile([P, P], F32, name="ident")
+        make_identity(nc, ident[:])
+        warm = keep.tile([P, 1], F32, name="warm")
+        nc.vector.memset(warm[:], 0.0)
+        nc.scalar.activation(out=warm[:], in_=warm[:], func=ACT.Sigmoid)
+
+        h_rows = keep.tile([P, CH], BF16, name="h_rows")
+        nc.sync.dma_start(out=h_rows[:], in_=h_tilde[:, :])
+        z_rows = keep.tile([P, SIZE], BF16, name="z_rows")
+        nc.sync.dma_start(out=z_rows[:], in_=z0[:, :])
+        for g in range(GATES):
+            nc.sync.dma_start(
+                out=bias_rows[g : g + 1, :], in_=b_dram[g].rearrange("(o c) -> o c", o=1)
+            )
+        u_rows = []
+        w_rows = []
+        for g in range(GATES):
+            rows = keep.tile([P, ROW_BLOCKS * CH], BF16, name="u_rows_%d" % g)
+            nc.sync.dma_start(
+                out=rows[:], in_=u_dram[g].rearrange("(p b) k -> p (b k)", b=ROW_BLOCKS)
+            )
+            u_rows.append(rows)
+            rows = keep.tile([P, ROW_BLOCKS * SIZE], BF16, name="w_rows_%d" % g)
+            if g < GATES - 1:
+                nc.sync.dma_start(
+                    out=rows[:], in_=w_dram[g].rearrange("(p b) k -> p (b k)", b=ROW_BLOCKS)
+                )
+            else:
+                for b in range(ROW_BLOCKS):
+                    nc.sync.dma_start(
+                        out=rows[:, b * SIZE : (b + 1) * SIZE],
+                        in_=w_dram[g].rearrange("(p b) k -> p b k", b=ROW_BLOCKS)[:, b, :],
+                    )
+            w_rows.append(rows)
+        fc = keep.tile([P, CH], BF16, name="fc")
+        nc.sync.dma_start(out=fc[:], in_=fc_sum[:, :])
+
+        bank = transpose_words(nc, banks, word_blocks(h_rows[:]), ident)
+        h_pairs = keep.tile([P, P], F32, name="h_pairs")
+        nc.vector.tensor_copy(out=h_pairs[:], in_=bank[:, 0, :])
+
+        z_codes = keep.tile([P, WORDS], U32, align_bytes=64, name="z_codes")
+        z_scales = keep.tile([P, WORDS], U8, align_bytes=64, name="z_scales")
+        z_bank = transpose_words(nc, banks, alternate_blocks(z_rows[:]), ident)
+        bank = transpose_words(nc, banks, word_blocks(bias_rows[:]), ident)
+        bias_cols = keep.tile([P, GATES], F32, name="bias_cols")
+        nc.vector.tensor_copy(out=bias_cols[:], in_=bank[:, 0, 0:GATES])
+        pack_rows(nc, stage, z_bank, z_codes[:], z_scales[:])
+        bank = transpose_words(
+            nc, banks, [bias_cols[:, g : g + 1].to_broadcast([P, P]) for g in range(GATES)], ident
+        )
+        bias_all = keep.tile([P, GATES * CH], BF16, name="bias_all")
+        nc.vector.tensor_copy(
+            out=bias_all[:].bitcast(F32).rearrange("p (g w) -> p g w", g=GATES),
+            in_=bank[:, 0:GATES, :],
+        )
+
+        w_codes = keep.tile([P, GATES * ROW_BLOCKS, WORDS], U32, align_bytes=64, name="w_codes")
+        w_scales = keep.tile([P, GATES * ROW_BLOCKS, WORDS], U8, align_bytes=64, name="w_scales")
+        def transposed_u(g):
+            bank = transpose_words(nc, banks, word_blocks(u_rows[g][:]), ident)
+            pairs = keep.tile([P, CH], F32, name="u_pairs_%d" % g)
+            nc.vector.tensor_copy(
+                out=pairs[:].rearrange("p (b r) -> p b r", b=ROW_BLOCKS),
+                in_=bank[:, 0:ROW_BLOCKS, :],
+            )
+            return pairs
+
+        plain = []
+        u_pairs = [transposed_u(0)]
+        for g in range(GATES):
+            w_blocks = [
+                block
+                for b in range(ROW_BLOCKS)
+                for block in alternate_blocks(w_rows[g][:, b * SIZE : (b + 1) * SIZE])
+            ]
+            per_block = len(w_blocks) // ROW_BLOCKS
+            j = g * ROW_BLOCKS
+            w_bank = transpose_words(nc, banks, w_blocks[0:per_block], ident)
+            if g + 1 < GATES:
+                u_pairs.append(transposed_u(g + 1))
+            pack_rows(nc, stage, w_bank, w_codes[:, j, :], w_scales[:, j, :])
+            w_bank = transpose_words(nc, banks, w_blocks[per_block : 2 * per_block], ident)
+            plain_ps = sums.tile([P, CH], F32, tag="sums", name="plain_ps")
+            for e in range(2):
+                nc.tensor.matmul(
+                    out=plain_ps[:],
+                    lhsT=by_parity(h_pairs, e),
+                    rhs=by_parity(u_pairs[g], e),
+                    start=(e == 0),
+                    stop=(e == 1),
+                )
+            plain_sb = keep.tile([P, CH], F32, name="plain_%d" % g)
+            nc.vector.tensor_tensor(
+                out=channels(plain_sb[:]),
+                in0=from_blocks(plain_ps[:]),
+                in1=channels(bias_all[:, g * CH : (g + 1) * CH]),
+                op=ALU.add,
+            )
+            plain.append(plain_sb)
+            pack_rows(nc, stage, w_bank, w_codes[:, j + 1, :], w_scales[:, j + 1, :])
+
+        acts = []
+        for g in range(GATES):
+            mx_ps = sums.tile([P, CH], F32, tag="sums", name="mx_ps")
+            for b in range(ROW_BLOCKS):
+                j = g * ROW_BLOCKS + b
+                for k_pass in range(PASSES):
+                    cols = slice(k_pass * P, (k_pass + 1) * P)
+                    nc.tensor.matmul_mx(
+                        out=mx_ps[:, b * P : (b + 1) * P],
+                        lhsT=z_codes[:, cols].bitcast(FP8X4),
+                        lhsT_scale=z_scales[:, cols],
+                        rhs=w_codes[:, j, cols].bitcast(FP8X4),
+                        rhs_scale=w_scales[:, j, cols],
+                        start=(k_pass == 0),
+                        stop=(k_pass == PASSES - 1),
+                    )
+            pre = keep.tile([P, CH], F32, name="pre_%d" % g)
+            nc.vector.tensor_tensor(
+                out=channels(pre[:]), in0=from_blocks(mx_ps[:]), in1=channels(plain[g][:]), op=ALU.add
+            )
+            act = keep.tile([P, CH], F32, name="act_%d" % g)
+            nc.scalar.activation(out=act[:], in_=pre[:], func=gate_func[g])
+            acts.append(act)
+        act_i, act_u, act_o = acts
+
+        c_sb = keep.tile([P, CH], F32, name="c_sb")
+        nc.vector.tensor_tensor(out=c_sb[:], in0=act_i[:], in1=act_u[:], op=ALU.mult)
+        nc.vector.tensor_tensor(out=c_sb[:], in0=c_sb[:], in1=fc[:], op=ALU.add)
+        nc.sync.dma_start(out=out[:, CH : 2 * CH], in_=c_sb[:])
+        tanh_c = keep.tile([P, CH], F32, name="tanh_c")
+        nc.scalar.activation(out=tanh_c[:], in_=c_sb[:], func=ACT.Tanh)
+        h_sb = keep.tile([P, CH], F32, name="h_sb")
+        nc.vector.tensor_tensor(out=h_sb[:], in0=act_o[:], in1=tanh_c[:], op=ALU.mult)
+        nc.sync.dma_start(out=out[:, 0:CH], in_=h_sb[:])

@@ -15,71 +15,43 @@ P = 128
 SIZE = 1024
 CH = 256
 GATES = 3
-ROW_BLOCKS = CH // P
 PASSES = SIZE // (4 * P)
-HALVES = 2
+K_PASS = 4 * P
 WORDS = PASSES * P
-BANK_SLOTS = 4
 
 FLOPS = 2 * P * GATES * CH * (SIZE + CH)
 
 
-def word_blocks(rows):
+def adjacent_words(rows):
     words = rows.bitcast(F32)
     return [words[:, s * P : (s + 1) * P] for s in range(words.shape[1] // P)]
 
 
-def alternate_blocks(rows):
+def alternate_words(rows):
     words = rows.bitcast(F32)
+    n = 2 * P
     return [
-        words[:, 2 * P * g + half : 2 * P * (g + 1) : 2]
-        for g in range(PASSES)
-        for half in range(HALVES)
+        words[:, n * g + half : n * (g + 1) : 2]
+        for g in range(words.shape[1] // n)
+        for half in range(2)
     ]
 
 
-def transpose_words(nc, banks, blocks, ident):
-    bank = banks.tile([P, BANK_SLOTS, P], F32, tag="bank", name="bank")
-    for slot in range(len(blocks)):
-        nc.tensor.transpose(out=bank[:, slot, :], in_=blocks[slot], identity=ident[:])
-    return bank
-
-
-def pack_rows(nc, stage, bank, codes, scales):
-    grouped = stage.tile([P, SIZE], BF16, align_bytes=64, name="grouped")
-    nc.scalar.copy(
-        out=grouped[:].bitcast(F32).rearrange("p (g r u) -> p g r u", g=PASSES, u=HALVES),
-        in_=bank[:].rearrange("p (g u) r -> p g r u", u=HALVES),
-    )
-    nc.vector.quantize_mx(out=codes.bitcast(FP8X4), scales=scales, in_=grouped[:])
-
-
 def by_parity(pairs, e):
-    return pairs[:].bitcast(BF16).rearrange("p (c e) -> p c e", e=2)[:, :, e]
-
-
-def from_blocks(sums_ps):
-    return sums_ps.rearrange("p (b r) -> p r b", b=ROW_BLOCKS)
-
-
-def channels(ap):
-    return ap.rearrange("p (r b) -> p r b", b=ROW_BLOCKS)
+    return pairs.bitcast(BF16).rearrange("p (c e) -> p c e", e=2)[:, :, e]
 
 
 def tile_treelstm_pb_s_kernel(
     tc, z0, h_tilde, fc_sum, W_i, U_i, b_i, W_o, U_o, b_o, W_u, U_u, b_u, out
 ):
     nc = tc.nc
-    w_dram = (W_i, W_u, W_o)
-    u_dram = (U_i, U_u, U_o)
-    b_dram = (b_i, b_u, b_o)
-    gate_func = (ACT.Sigmoid, ACT.Tanh, ACT.Sigmoid)
-
+    w_dram = {"i": W_i, "u": W_u, "o": W_o}
+    u_dram = {"i": U_i, "u": U_u, "o": U_o}
+    b_dram = {"i": b_i, "u": b_u, "o": b_o}
     with ExitStack() as ctx:
         keep = ctx.enter_context(tc.tile_pool(name="keep", bufs=1))
-        stage = ctx.enter_context(tc.tile_pool(name="stage", bufs=4))
-        banks = ctx.enter_context(tc.psum_pool(name="banks", bufs=5))
-        sums = ctx.enter_context(tc.psum_pool(name="sums", bufs=GATES))
+        banks = ctx.enter_context(tc.psum_pool(name="banks", bufs=4))
+        sums = ctx.enter_context(tc.psum_pool(name="sums", bufs=4))
         ctx.enter_context(tc.manual_schedule())
 
         bias_rows = keep.tile([P, CH], BF16, name="bias_rows")
@@ -91,132 +63,264 @@ def tile_treelstm_pb_s_kernel(
         nc.scalar.activation(out=warm[:], in_=warm[:], func=ACT.Sigmoid)
 
         h_rows = keep.tile([P, CH], BF16, name="h_rows")
-        nc.sync.dma_start(out=h_rows[:], in_=h_tilde[:, :])
         z_rows = keep.tile([P, SIZE], BF16, name="z_rows")
-        nc.sync.dma_start(out=z_rows[:], in_=z0[:, :])
-        for g in range(GATES):
-            nc.sync.dma_start(
-                out=bias_rows[g : g + 1, :], in_=b_dram[g].rearrange("(o c) -> o c", o=1)
-            )
-        u_rows = []
-        w_rows = []
-        for g in range(GATES):
-            rows = keep.tile([P, ROW_BLOCKS * CH], BF16, name="u_rows_%d" % g)
-            nc.sync.dma_start(
-                out=rows[:], in_=u_dram[g].rearrange("(p b) k -> p (b k)", b=ROW_BLOCKS)
-            )
-            u_rows.append(rows)
-            rows = keep.tile([P, ROW_BLOCKS * SIZE], BF16, name="w_rows_%d" % g)
-            if g < GATES - 1:
-                nc.sync.dma_start(
-                    out=rows[:], in_=w_dram[g].rearrange("(p b) k -> p (b k)", b=ROW_BLOCKS)
-                )
-            else:
-                for b in range(ROW_BLOCKS):
-                    nc.sync.dma_start(
-                        out=rows[:, b * SIZE : (b + 1) * SIZE],
-                        in_=w_dram[g].rearrange("(p b) k -> p b k", b=ROW_BLOCKS)[:, b, :],
-                    )
-            w_rows.append(rows)
         fc = keep.tile([P, CH], BF16, name="fc")
-        nc.sync.dma_start(out=fc[:], in_=fc_sum[:, :])
-
-        bank = transpose_words(nc, banks, word_blocks(h_rows[:]), ident)
         h_pairs = keep.tile([P, P], F32, name="h_pairs")
-        nc.vector.tensor_copy(out=h_pairs[:], in_=bank[:, 0, :])
-
-        z_codes = keep.tile([P, WORDS], U32, align_bytes=64, name="z_codes")
-        z_scales = keep.tile([P, WORDS], U8, align_bytes=64, name="z_scales")
-        z_bank = transpose_words(nc, banks, alternate_blocks(z_rows[:]), ident)
-        bank = transpose_words(nc, banks, word_blocks(bias_rows[:]), ident)
         bias_cols = keep.tile([P, GATES], F32, name="bias_cols")
-        nc.vector.tensor_copy(out=bias_cols[:], in_=bank[:, 0, 0:GATES])
-        pack_rows(nc, stage, z_bank, z_codes[:], z_scales[:])
-        bank = transpose_words(
-            nc, banks, [bias_cols[:, g : g + 1].to_broadcast([P, P]) for g in range(GATES)], ident
-        )
         bias_all = keep.tile([P, GATES * CH], BF16, name="bias_all")
-        nc.vector.tensor_copy(
-            out=bias_all[:].bitcast(F32).rearrange("p (g w) -> p g w", g=GATES),
-            in_=bank[:, 0:GATES, :],
-        )
+        c_sb = keep.tile([P, CH], F32, name="c_sb")
+        rows, grouped, codes, scales, ps, pairs, t, pre, act, held = {}, {}, {}, {}, {}, {}, {}, {}, {}, {}
 
-        w_codes = keep.tile([P, GATES * ROW_BLOCKS, WORDS], U32, align_bytes=64, name="w_codes")
-        w_scales = keep.tile([P, GATES * ROW_BLOCKS, WORDS], U8, align_bytes=64, name="w_scales")
-        def transposed_u(g):
-            bank = transpose_words(nc, banks, word_blocks(u_rows[g][:]), ident)
-            pairs = keep.tile([P, CH], F32, name="u_pairs_%d" % g)
+        def load_h():
+            nc.sync.dma_start(out=h_rows[:], in_=h_tilde[:, :])
+
+        def load_z():
+            nc.sync.dma_start(out=z_rows[:], in_=z0[:, :])
+            rows["z"] = z_rows[:]
+
+        def load_fc():
+            nc.sync.dma_start(out=fc[:], in_=fc_sum[:, :])
+
+        def load_b(engine=None):
+            for j, g in enumerate("iuo"):
+                (engine or nc.sync).dma_start(
+                    out=bias_rows[j : j + 1, :], in_=b_dram[g].rearrange("(o c) -> o c", o=1)
+                )
+
+        def load_u(g):
+            tile = keep.tile([P, 2 * CH], BF16, name="u_rows_" + g)
+            nc.sync.dma_start(out=tile[:], in_=u_dram[g].rearrange("(p b) k -> p (b k)", b=2))
+            rows["U" + g] = tile[:]
+
+        def load_w(g, b):
+            tile = keep.tile([P, SIZE], BF16, name="w_rows_%s%d" % (g, b))
+            nc.sync.dma_start(out=tile[:], in_=w_dram[g][b * P : (b + 1) * P, :])
+            rows["%s%d" % (g, b)] = tile[:]
+
+        def load_w2(g):
+            tile = keep.tile([P, 2 * SIZE], BF16, name="w_rows_" + g)
+            nc.sync.dma_start(out=tile[:], in_=w_dram[g].rearrange("(p b) k -> p (b k)", b=2))
+            for b in range(2):
+                rows["%s%d" % (g, b)] = tile[:, b * SIZE : (b + 1) * SIZE]
+            paired.add(g)
+
+        def flip(n, blocks):
+            bank = banks.tile([P, 4, P], F32, tag="bank", name="bank")
+            for slot in range(len(blocks)):
+                nc.tensor.transpose(out=bank[:, slot, :], in_=blocks[slot], identity=ident[:])
+            held[n] = bank
+
+        def flip_h():
+            flip("h", adjacent_words(h_rows[:]))
+
+        def copy_h():
+            nc.vector.tensor_copy(out=h_pairs[:], in_=held["h"][:, 0, :])
+
+        def flip_b():
+            flip("b", adjacent_words(bias_rows[:]))
+
+        def copy_b():
+            nc.vector.tensor_copy(out=bias_cols[:], in_=held["b"][:, 0, 0:GATES])
+
+        def spread_b():
+            flip("bb", [bias_cols[:, g : g + 1].to_broadcast([P, P]) for g in range(GATES)])
+
+        def copy_bb():
             nc.vector.tensor_copy(
-                out=pairs[:].rearrange("p (b r) -> p b r", b=ROW_BLOCKS),
-                in_=bank[:, 0:ROW_BLOCKS, :],
+                out=bias_all[:].bitcast(F32).rearrange("p (g w) -> p g w", g=GATES),
+                in_=held["bb"][:, 0:GATES, :],
             )
-            return pairs
 
-        plain = []
-        u_pairs = [transposed_u(0)]
-        for g in range(GATES):
-            w_blocks = [
-                block
-                for b in range(ROW_BLOCKS)
-                for block in alternate_blocks(w_rows[g][:, b * SIZE : (b + 1) * SIZE])
-            ]
-            per_block = len(w_blocks) // ROW_BLOCKS
-            j = g * ROW_BLOCKS
-            w_bank = transpose_words(nc, banks, w_blocks[0:per_block], ident)
-            if g + 1 < GATES:
-                u_pairs.append(transposed_u(g + 1))
-            pack_rows(nc, stage, w_bank, w_codes[:, j, :], w_scales[:, j, :])
-            w_bank = transpose_words(nc, banks, w_blocks[per_block : 2 * per_block], ident)
-            plain_ps = sums.tile([P, CH], F32, tag="sums", name="plain_ps")
+        def flip_u(g):
+            flip("U" + g, adjacent_words(rows["U" + g]))
+
+        def copy_u(g, copy):
+            tile = keep.tile([P, CH], F32, name="pairs_" + g)
+            copy(
+                out=tile[:].rearrange("p (r b) -> p r b", b=2),
+                in_=held["U" + g][:, 0:2, :].rearrange("p b r -> p r b"),
+            )
+            pairs[g] = tile
+
+        def plain(g):
+            acc = sums.tile([P, CH], F32, tag="sums", name="plain_ps")
             for e in range(2):
                 nc.tensor.matmul(
-                    out=plain_ps[:],
-                    lhsT=by_parity(h_pairs, e),
-                    rhs=by_parity(u_pairs[g], e),
+                    out=acc[:],
+                    lhsT=by_parity(h_pairs[:], e),
+                    rhs=by_parity(pairs[g][:], e),
                     start=(e == 0),
                     stop=(e == 1),
                 )
-            plain_sb = keep.tile([P, CH], F32, name="plain_%d" % g)
-            nc.vector.tensor_tensor(
-                out=channels(plain_sb[:]),
-                in0=from_blocks(plain_ps[:]),
-                in1=channels(bias_all[:, g * CH : (g + 1) * CH]),
-                op=ALU.add,
-            )
-            plain.append(plain_sb)
-            pack_rows(nc, stage, w_bank, w_codes[:, j + 1, :], w_scales[:, j + 1, :])
+            ps["plain_" + g] = acc
 
-        acts = []
-        for g in range(GATES):
-            mx_ps = sums.tile([P, CH], F32, tag="sums", name="mx_ps")
-            for b in range(ROW_BLOCKS):
-                j = g * ROW_BLOCKS + b
+        def add_bias(g):
+            tile = keep.tile([P, CH], F32, name="t_" + g)
+            j = "iuo".index(g)
+            nc.vector.tensor_tensor(
+                out=tile[:], in0=ps["plain_" + g][:], in1=bias_all[:, j * CH : (j + 1) * CH], op=ALU.add
+            )
+            t[g] = tile
+
+        def flip_w(n, passes=range(PASSES)):
+            first, last = passes[0], passes[-1] + 1
+            flip((n, first), alternate_words(rows[n][:, first * K_PASS : last * K_PASS]))
+
+        def copy_w(n, copy, passes=range(PASSES)):
+            first, count = passes[0], len(passes)
+            if n not in grouped:
+                grouped[n] = keep.tile([P, SIZE], BF16, align_bytes=64, name="grouped_" + n)
+            copy(
+                out=grouped[n][:, first * K_PASS : (first + count) * K_PASS]
+                .bitcast(F32)
+                .rearrange("p (g r u) -> p g r u", g=count, u=2),
+                in_=held[(n, first)][:, 0 : 2 * count, :].rearrange("p (g u) r -> p g r u", u=2),
+            )
+
+        def quantise(n, passes=range(PASSES)):
+            first, count = passes[0], len(passes)
+            if n not in codes:
+                codes[n] = keep.tile([P, WORDS], U32, align_bytes=64, name="codes_" + n)
+                scales[n] = keep.tile([P, WORDS], U8, align_bytes=64, name="scales_" + n)
+            cols = slice(first * P, (first + count) * P)
+            nc.vector.quantize_mx(
+                out=codes[n][:, cols].bitcast(FP8X4),
+                scales=scales[n][:, cols],
+                in_=grouped[n][:, first * K_PASS : (first + count) * K_PASS],
+            )
+
+        def products(g, blocks):
+            acc = sums.tile([P, len(blocks) * P], F32, tag="sums", name="mx_ps")
+            for i in range(len(blocks)):
+                n = "%s%d" % (g, blocks[i])
                 for k_pass in range(PASSES):
                     cols = slice(k_pass * P, (k_pass + 1) * P)
                     nc.tensor.matmul_mx(
-                        out=mx_ps[:, b * P : (b + 1) * P],
-                        lhsT=z_codes[:, cols].bitcast(FP8X4),
-                        lhsT_scale=z_scales[:, cols],
-                        rhs=w_codes[:, j, cols].bitcast(FP8X4),
-                        rhs_scale=w_scales[:, j, cols],
+                        out=acc[:, i * P : (i + 1) * P],
+                        lhsT=codes["z"][:, cols].bitcast(FP8X4),
+                        lhsT_scale=scales["z"][:, cols],
+                        rhs=codes[n][:, cols].bitcast(FP8X4),
+                        rhs_scale=scales[n][:, cols],
                         start=(k_pass == 0),
                         stop=(k_pass == PASSES - 1),
                     )
-            pre = keep.tile([P, CH], F32, name="pre_%d" % g)
-            nc.vector.tensor_tensor(
-                out=channels(pre[:]), in0=from_blocks(mx_ps[:]), in1=channels(plain[g][:]), op=ALU.add
-            )
-            act = keep.tile([P, CH], F32, name="act_%d" % g)
-            nc.scalar.activation(out=act[:], in_=pre[:], func=gate_func[g])
-            acts.append(act)
-        act_i, act_u, act_o = acts
+                ps[n] = (acc, i)
 
-        c_sb = keep.tile([P, CH], F32, name="c_sb")
-        nc.vector.tensor_tensor(out=c_sb[:], in0=act_i[:], in1=act_u[:], op=ALU.mult)
-        nc.vector.tensor_tensor(out=c_sb[:], in0=c_sb[:], in1=fc[:], op=ALU.add)
-        nc.sync.dma_start(out=out[:, CH : 2 * CH], in_=c_sb[:])
-        tanh_c = keep.tile([P, CH], F32, name="tanh_c")
-        nc.scalar.activation(out=tanh_c[:], in_=c_sb[:], func=ACT.Tanh)
+        def span(blocks):
+            return slice(blocks[0] * P, (blocks[-1] + 1) * P)
+
+        def add_mx(g, blocks):
+            if g not in pre:
+                pre[g] = keep.tile([P, CH], F32, name="pre_" + g)
+            acc = ps["%s%d" % (g, blocks[0])][0]
+            views = [pre[g][:, span(blocks)], acc[:], t[g][:, span(blocks)]]
+            if g in paired:
+                views[0] = views[0].rearrange("p (r b) -> p r b", b=2)
+                views[1] = views[1].rearrange("p (b r) -> p r b", b=2)
+                views[2] = views[2].rearrange("p (r b) -> p r b", b=2)
+            nc.vector.tensor_tensor(out=views[0], in0=views[1], in1=views[2], op=ALU.add)
+
+        def activate(g, blocks):
+            if g not in act:
+                act[g] = keep.tile([P, CH], F32, name="act_" + g)
+            source = c_sb if g == "c" else pre[g]
+            nc.scalar.activation(
+                out=act[g][:, span(blocks)],
+                in_=source[:, span(blocks)],
+                func=ACT.Tanh if g in "uc" else ACT.Sigmoid,
+            )
+
+        paired = set()
+        prod = keep.tile([P, CH], F32, name="prod")
         h_sb = keep.tile([P, CH], F32, name="h_sb")
-        nc.vector.tensor_tensor(out=h_sb[:], in0=act_o[:], in1=tanh_c[:], op=ALU.mult)
-        nc.sync.dma_start(out=out[:, 0:CH], in_=h_sb[:])
+
+        def times_iu(blocks):
+            s = span(blocks)
+            nc.vector.tensor_tensor(out=prod[:, s], in0=act["i"][:, s], in1=act["u"][:, s], op=ALU.mult)
+
+        def add_fc(blocks):
+            s = span(blocks)
+            nc.vector.tensor_tensor(out=c_sb[:, s], in0=prod[:, s], in1=fc[:, s], op=ALU.add)
+
+        def store_c():
+            nc.sync.dma_start(out=out[:, CH : 2 * CH], in_=c_sb[:])
+
+        def times_o(blocks):
+            s = span(blocks)
+            nc.vector.tensor_tensor(out=h_sb[:, s], in0=act["o"][:, s], in1=act["c"][:, s], op=ALU.mult)
+            nc.sync.dma_start(out=out[:, s], in_=h_sb[:, s])
+
+        by_s, by_v = nc.scalar.copy, nc.vector.tensor_copy
+        both = (0, 1)
+        load_h()
+        load_z()
+        load_b()
+        load_u("i")
+        load_w2("i")
+        load_u("u")
+        load_w2("u")
+        load_u("o")
+        load_w("o",0)
+        load_w("o",1)
+        load_fc()
+        flip_h()
+        copy_h()
+        flip_w("z")
+        copy_w("z",by_s)
+        flip_b()
+        copy_b()
+        flip_u("i")
+        copy_u("i",by_s)
+        spread_b()
+        quantise("z")
+        copy_bb()
+        flip_w("i0")
+        copy_w("i0",by_s)
+        flip_u("u")
+        copy_u("u",by_s)
+        flip_w("i1")
+        copy_w("i1",by_s)
+        quantise("i0")
+        quantise("i1")
+        flip_w("u0")
+        copy_w("u0",by_s)
+        flip_u("o")
+        copy_u("o",by_s)
+        flip_w("u1")
+        copy_w("u1",by_s)
+        quantise("u0")
+        flip_w("o0")
+        copy_w("o0",by_s)
+        plain("i")
+        add_bias("i")
+        plain("u")
+        quantise("u1")
+        add_bias("u")
+        flip_w("o1")
+        copy_w("o1",by_s)
+        quantise("o0")
+        products("i",both)
+        add_mx("i",both)
+        activate("i",both)
+        products("u",both)
+        add_mx("u",both)
+        activate("u",(0,))
+        activate("u",(1,))
+        plain("o")
+        products("o",(0,))
+        add_bias("o")
+        quantise("o1")
+        products("o",(1,))
+        add_mx("o",(0,))
+        activate("o",(0,))
+        times_iu((0,))
+        times_iu((1,))
+        add_fc((0,))
+        activate("c",(0,))
+        add_fc((1,))
+        activate("c",(1,))
+        store_c()
+        add_mx("o",(1,))
+        activate("o",(1,))
+        times_o((0,))
+        times_o((1,))

@@ -253,11 +253,11 @@ def tile_treelstm_pb_s_kernel(
         by_s, by_v = nc.scalar.copy, nc.vector.tensor_copy
         both = (0, 1)
         load_h()
+        load_u("i")
         load_z()
         load_b()
-        load_u("i")
-        load_w2("i")
         load_u("u")
+        load_w2("i")
         load_w2("u")
         load_u("o")
         load_w("o",0)
@@ -265,37 +265,39 @@ def tile_treelstm_pb_s_kernel(
         load_fc()
         flip_h()
         copy_h()
+        flip_u("i")
+        copy_u("i",by_s)
         flip_w("z")
         copy_w("z",by_s)
         flip_b()
         copy_b()
-        flip_u("i")
-        copy_u("i",by_s)
+        plain("i")
+        flip_u("u")
+        copy_u("u",by_s)
         spread_b()
         quantise("z")
         copy_bb()
+        add_bias("i")
         flip_w("i0")
         copy_w("i0",by_s)
-        flip_u("u")
-        copy_u("u",by_s)
         flip_w("i1")
         copy_w("i1",by_s)
+        plain("u")
+        add_bias("u")
         quantise("i0")
         quantise("i1")
         flip_w("u0")
         copy_w("u0",by_s)
         flip_u("o")
-        copy_u("o",by_s)
+        copy_u("o",by_v)
         flip_w("u1")
         copy_w("u1",by_s)
         quantise("u0")
         flip_w("o0")
         copy_w("o0",by_s)
-        plain("i")
-        add_bias("i")
-        plain("u")
+        plain("o")
+        add_bias("o")
         quantise("u1")
-        add_bias("u")
         flip_w("o1")
         copy_w("o1",by_s)
         quantise("o0")
@@ -306,9 +308,7 @@ def tile_treelstm_pb_s_kernel(
         add_mx("u",both)
         activate("u",(0,))
         activate("u",(1,))
-        plain("o")
         products("o",(0,))
-        add_bias("o")
         quantise("o1")
         products("o",(1,))
         add_mx("o",(0,))

@@ -54,13 +54,14 @@ def tile_treelstm_pb_s_kernel(
         sums = ctx.enter_context(tc.psum_pool(name="sums", bufs=4))
         ctx.enter_context(tc.manual_schedule())
 
+        warm = keep.tile([P, P], F32, name="warm")
+        nc.vector.memset(warm[:], 0.0)
         bias_rows = keep.tile([P, CH], BF16, name="bias_rows")
         nc.vector.memset(bias_rows[:], 0.0)
         ident = keep.tile([P, P], F32, name="ident")
         make_identity(nc, ident[:])
-        warm = keep.tile([P, 1], F32, name="warm")
-        nc.vector.memset(warm[:], 0.0)
-        nc.scalar.activation(out=warm[:], in_=warm[:], func=ACT.Sigmoid)
+        warm_act = keep.tile([P, 1], F32, name="warm_act")
+        nc.scalar.activation(out=warm_act[:], in_=warm[:, 0:1], func=ACT.Sigmoid)
 
         h_rows = keep.tile([P, CH], BF16, name="h_rows")
         z_rows = keep.tile([P, SIZE], BF16, name="z_rows")
@@ -263,6 +264,11 @@ def tile_treelstm_pb_s_kernel(
         load_w("o",0)
         load_w("o",1)
         load_fc()
+        warm_ps = sums.tile([P, CH], F32, tag="sums", name="warm_ps")
+        for i in range(3):
+            nc.tensor.matmul(
+                out=warm_ps[:, 0:P], lhsT=warm[:], rhs=warm[:], start=True, stop=True
+            )
         flip_h()
         copy_h()
         flip_u("i")

@@ -265,13 +265,18 @@ def tile_treelstm_pb_s_kernel(
         load_w("o",1)
         load_fc()
         warm_ps = sums.tile([P, CH], F32, tag="sums", name="warm_ps")
-        for i in range(3):
+
+        def keep_warm():
             nc.tensor.matmul(
-                out=warm_ps[:, 0:P], lhsT=warm[:], rhs=warm[:], start=True, stop=True
+                out=warm_ps[:, 0:96], lhsT=warm[:], rhs=warm[:, 0:96], start=True, stop=True
             )
+
+        for i in range(3):
+            keep_warm()
         flip_h()
         copy_h()
         flip_u("i")
+        keep_warm()
         copy_u("i",by_s)
         flip_w("z")
         copy_w("z",by_s)

@@ -260,9 +260,9 @@ def tile_treelstm_pb_s_kernel(
         load_u("u")
         load_w2("i")
         load_w2("u")
-        load_u("o")
         load_w("o",0)
         load_w("o",1)
+        load_u("o")
         load_fc()
         warm_ps = sums.tile([P, CH], F32, tag="sums", name="warm_ps")
 
@@ -293,39 +293,42 @@ def tile_treelstm_pb_s_kernel(
         copy_w("i0",by_s)
         flip_w("i1")
         copy_w("i1",by_s)
-        plain("u")
-        add_bias("u")
         quantise("i0")
         quantise("i1")
         flip_w("u0")
         copy_w("u0",by_s)
-        flip_u("o")
-        copy_u("o",by_v)
+        plain("u")
+        add_bias("u")
         flip_w("u1")
         copy_w("u1",by_s)
         quantise("u0")
         flip_w("o0")
         copy_w("o0",by_s)
-        plain("o")
-        add_bias("o")
         quantise("u1")
-        flip_w("o1")
-        copy_w("o1",by_s)
+        flip_w("o1",(0,))
+        flip_w("o1",(1,))
+        copy_w("o1",by_s,(0,))
+        flip_u("o")
+        copy_w("o1",by_s,(1,))
         quantise("o0")
         products("i",both)
         add_mx("i",both)
+        copy_u("o",by_s)
         activate("i",both)
         products("u",both)
         add_mx("u",both)
         activate("u",(0,))
         activate("u",(1,))
         products("o",(0,))
-        quantise("o1")
+        plain("o")
+        quantise("o1",(0,))
+        quantise("o1",(1,))
+        add_bias("o")
         products("o",(1,))
-        add_mx("o",(0,))
-        activate("o",(0,))
         times_iu((0,))
         times_iu((1,))
+        add_mx("o",(0,))
+        activate("o",(0,))
         add_fc((0,))
         activate("c",(0,))
         add_fc((1,))

@@ -143,17 +143,17 @@ def tile_treelstm_pb_s_kernel(
             )
             pairs[g] = tile
 
-        def plain(g):
-            acc = sums.tile([P, CH], F32, tag="sums", name="plain_ps")
-            for e in range(2):
+        def plain(g, parities=(0, 1)):
+            if 0 in parities:
+                ps["plain_" + g] = sums.tile([P, CH], F32, tag="sums", name="plain_ps")
+            for e in parities:
                 nc.tensor.matmul(
-                    out=acc[:],
+                    out=ps["plain_" + g][:],
                     lhsT=by_parity(h_pairs[:], e),
                     rhs=by_parity(pairs[g][:], e),
                     start=(e == 0),
                     stop=(e == 1),
                 )
-            ps["plain_" + g] = acc
 
         def add_bias(g):
             tile = keep.tile([P, CH], F32, name="t_" + g)
@@ -282,26 +282,28 @@ def tile_treelstm_pb_s_kernel(
         copy_w("z",by_s)
         flip_b()
         copy_b()
-        plain("i")
+        plain("i",(0,))
         flip_u("u")
         copy_u("u",by_s)
         spread_b()
         quantise("z")
         copy_bb()
+        plain("i",(1,))
         add_bias("i")
         flip_w("i0")
         copy_w("i0",by_s)
         flip_w("i1")
         copy_w("i1",by_s)
+        plain("u",(0,))
         quantise("i0")
         quantise("i1")
         flip_w("u0")
         copy_w("u0",by_s)
-        plain("u")
-        add_bias("u")
         flip_w("u1")
         copy_w("u1",by_s)
+        plain("u",(1,))
         quantise("u0")
+        add_bias("u")
         flip_w("o0")
         copy_w("o0",by_s)
         quantise("u1")

from contextlib import ExitStack

import concourse.mybir as mybir
from concourse.masks import make_identity

F32 = mybir.dt.float32
BF16 = mybir.dt.bfloat16
U32 = mybir.dt.uint32
U8 = mybir.dt.uint8
FP8X4 = mybir.dt.float8_e4m3fn_x4
ACT = mybir.ActivationFunctionType
ALU = mybir.AluOpType

P = 128
SIZE = 1024
CH = 256
GATES = 3
PASSES = SIZE // (4 * P)
K_PASS = 4 * P
WORDS = PASSES * P

FLOPS = 2 * P * GATES * CH * (SIZE + CH)


def adjacent_words(rows):
    words = rows.bitcast(F32)
    return [words[:, s * P : (s + 1) * P] for s in range(words.shape[1] // P)]


def alternate_words(rows):
    words = rows.bitcast(F32)
    n = 2 * P
    return [
        words[:, n * g + half : n * (g + 1) : 2]
        for g in range(words.shape[1] // n)
        for half in range(2)
    ]


def by_parity(pairs, e):
    return pairs.bitcast(BF16).rearrange("p (c e) -> p c e", e=2)[:, :, e]


def tile_treelstm_pb_s_kernel(
    tc, z0, h_tilde, fc_sum, W_i, U_i, b_i, W_o, U_o, b_o, W_u, U_u, b_u, out
):
    nc = tc.nc
    w_dram = {"i": W_i, "u": W_u, "o": W_o}
    u_dram = {"i": U_i, "u": U_u, "o": U_o}
    b_dram = {"i": b_i, "u": b_u, "o": b_o}
    with ExitStack() as ctx:
        keep = ctx.enter_context(tc.tile_pool(name="keep", bufs=1))
        banks = ctx.enter_context(tc.psum_pool(name="banks", bufs=4))
        sums = ctx.enter_context(tc.psum_pool(name="sums", bufs=4))
        ctx.enter_context(tc.manual_schedule())

        warm = keep.tile([P, P], F32, name="warm")
        nc.vector.memset(warm[:], 0.0)
        bias_rows = keep.tile([P, CH], BF16, name="bias_rows")
        nc.vector.memset(bias_rows[:], 0.0)
        ident = keep.tile([P, P], F32, name="ident")
        make_identity(nc, ident[:])
        warm_act = keep.tile([P, 1], F32, name="warm_act")
        nc.scalar.activation(out=warm_act[:], in_=warm[:, 0:1], func=ACT.Sigmoid)

        h_rows = keep.tile([P, CH], BF16, name="h_rows")
        z_rows = keep.tile([P, SIZE], BF16, name="z_rows")
        fc = keep.tile([P, CH], BF16, name="fc")
        h_pairs = keep.tile([P, P], F32, name="h_pairs")
        bias_cols = keep.tile([P, GATES], F32, name="bias_cols")
        bias_all = keep.tile([P, GATES * CH], BF16, name="bias_all")
        c_sb = keep.tile([P, CH], F32, name="c_sb")
        rows, grouped, codes, scales, ps, pairs, t, pre, act, held = {}, {}, {}, {}, {}, {}, {}, {}, {}, {}

        def load_h():
            nc.sync.dma_start(out=h_rows[:], in_=h_tilde[:, :])

        def load_z():
            nc.sync.dma_start(out=z_rows[:], in_=z0[:, :])
            rows["z"] = z_rows[:]

        def load_fc():
            nc.sync.dma_start(out=fc[:], in_=fc_sum[:, :])

        def load_b(engine=None):
            for j, g in enumerate("iuo"):
                (engine or nc.sync).dma_start(
                    out=bias_rows[j : j + 1, :], in_=b_dram[g].rearrange("(o c) -> o c", o=1)
                )

        def load_u(g):
            tile = keep.tile([P, 2 * CH], BF16, name="u_rows_" + g)
            nc.sync.dma_start(out=tile[:], in_=u_dram[g].rearrange("(p b) k -> p (b k)", b=2))
            rows["U" + g] = tile[:]

        def load_w(g, b):
            tile = keep.tile([P, SIZE], BF16, name="w_rows_%s%d" % (g, b))
            nc.sync.dma_start(out=tile[:], in_=w_dram[g][b * P : (b + 1) * P, :])
            rows["%s%d" % (g, b)] = tile[:]

        def load_w2(g):
            tile = keep.tile([P, 2 * SIZE], BF16, name="w_rows_" + g)
            nc.sync.dma_start(out=tile[:], in_=w_dram[g].rearrange("(p b) k -> p (b k)", b=2))
            for b in range(2):
                rows["%s%d" % (g, b)] = tile[:, b * SIZE : (b + 1) * SIZE]
            paired.add(g)

        def flip(n, blocks):
            bank = banks.tile([P, 4, P], F32, tag="bank", name="bank")
            for slot in range(len(blocks)):
                nc.tensor.transpose(out=bank[:, slot, :], in_=blocks[slot], identity=ident[:])
            held[n] = bank

        def flip_h():
            flip("h", adjacent_words(h_rows[:]))

        def copy_h():
            nc.vector.tensor_copy(out=h_pairs[:], in_=held["h"][:, 0, :])

        def flip_b():
            flip("b", adjacent_words(bias_rows[:]))

        def copy_b():
            nc.vector.tensor_copy(out=bias_cols[:], in_=held["b"][:, 0, 0:GATES])

        def spread_b():
            flip("bb", [bias_cols[:, g : g + 1].to_broadcast([P, P]) for g in range(GATES)])

        def copy_bb():
            nc.vector.tensor_copy(
                out=bias_all[:].bitcast(F32).rearrange("p (g w) -> p g w", g=GATES),
                in_=held["bb"][:, 0:GATES, :],
            )

        def flip_u(g):
            flip("U" + g, adjacent_words(rows["U" + g]))

        def copy_u(g, copy):
            tile = keep.tile([P, CH], F32, name="pairs_" + g)
            copy(
                out=tile[:].rearrange("p (r b) -> p r b", b=2),
                in_=held["U" + g][:, 0:2, :].rearrange("p b r -> p r b"),
            )
            pairs[g] = tile

        def plain(g, parities=(0, 1)):
            if 0 in parities:
                ps["plain_" + g] = sums.tile([P, CH], F32, tag="sums", name="plain_ps")
            for e in parities:
                nc.tensor.matmul(
                    out=ps["plain_" + g][:],
                    lhsT=by_parity(h_pairs[:], e),
                    rhs=by_parity(pairs[g][:], e),
                    start=(e == 0),
                    stop=(e == 1),
                )

        def add_bias(g):
            tile = keep.tile([P, CH], F32, name="t_" + g)
            j = "iuo".index(g)
            nc.vector.tensor_tensor(
                out=tile[:], in0=ps["plain_" + g][:], in1=bias_all[:, j * CH : (j + 1) * CH], op=ALU.add
            )
            t[g] = tile

        def flip_w(n, passes=range(PASSES)):
            first, last = passes[0], passes[-1] + 1
            flip((n, first), alternate_words(rows[n][:, first * K_PASS : last * K_PASS]))

        def copy_w(n, copy, passes=range(PASSES)):
            first, count = passes[0], len(passes)
            if n not in grouped:
                grouped[n] = keep.tile([P, SIZE], BF16, align_bytes=64, name="grouped_" + n)
            copy(
                out=grouped[n][:, first * K_PASS : (first + count) * K_PASS]
                .bitcast(F32)
                .rearrange("p (g r u) -> p g r u", g=count, u=2),
                in_=held[(n, first)][:, 0 : 2 * count, :].rearrange("p (g u) r -> p g r u", u=2),
            )

        def quantise(n, passes=range(PASSES)):
            first, count = passes[0], len(passes)
            if n not in codes:
                codes[n] = keep.tile([P, WORDS], U32, align_bytes=64, name="codes_" + n)
                scales[n] = keep.tile([P, WORDS], U8, align_bytes=64, name="scales_" + n)
            cols = slice(first * P, (first + count) * P)
            nc.vector.quantize_mx(
                out=codes[n][:, cols].bitcast(FP8X4),
                scales=scales[n][:, cols],
                in_=grouped[n][:, first * K_PASS : (first + count) * K_PASS],
            )

        def products(g, blocks):
            acc = sums.tile([P, len(blocks) * P], F32, tag="sums", name="mx_ps")
            for i in range(len(blocks)):
                n = "%s%d" % (g, blocks[i])
                for k_pass in range(PASSES):
                    cols = slice(k_pass * P, (k_pass + 1) * P)
                    nc.tensor.matmul_mx(
                        out=acc[:, i * P : (i + 1) * P],
                        lhsT=codes["z"][:, cols].bitcast(FP8X4),
                        lhsT_scale=scales["z"][:, cols],
                        rhs=codes[n][:, cols].bitcast(FP8X4),
                        rhs_scale=scales[n][:, cols],
                        start=(k_pass == 0),
                        stop=(k_pass == PASSES - 1),
                    )
                ps[n] = (acc, i)

        def span(blocks):
            return slice(blocks[0] * P, (blocks[-1] + 1) * P)

        def add_mx(g, blocks):
            if g not in pre:
                pre[g] = keep.tile([P, CH], F32, name="pre_" + g)
            acc = ps["%s%d" % (g, blocks[0])][0]
            views = [pre[g][:, span(blocks)], acc[:], t[g][:, span(blocks)]]
            if g in paired:
                views[0] = views[0].rearrange("p (r b) -> p r b", b=2)
                views[1] = views[1].rearrange("p (b r) -> p r b", b=2)
                views[2] = views[2].rearrange("p (r b) -> p r b", b=2)
            nc.vector.tensor_tensor(out=views[0], in0=views[1], in1=views[2], op=ALU.add)

        def activate(g, blocks):
            if g not in act:
                act[g] = keep.tile([P, CH], F32, name="act_" + g)
            source = c_sb if g == "c" else pre[g]
            nc.scalar.activation(
                out=act[g][:, span(blocks)],
                in_=source[:, span(blocks)],
                func=ACT.Tanh if g in "uc" else ACT.Sigmoid,
            )

        paired = set()
        prod = keep.tile([P, CH], F32, name="prod")
        h_sb = keep.tile([P, CH], F32, name="h_sb")

        def times_iu(blocks):
            s = span(blocks)
            nc.vector.tensor_tensor(out=prod[:, s], in0=act["i"][:, s], in1=act["u"][:, s], op=ALU.mult)

        def add_fc(blocks):
            s = span(blocks)
            nc.vector.tensor_tensor(out=c_sb[:, s], in0=prod[:, s], in1=fc[:, s], op=ALU.add)

        def store_c():
            nc.sync.dma_start(out=out[:, CH : 2 * CH], in_=c_sb[:])

        def times_o(blocks):
            s = span(blocks)
            nc.vector.tensor_tensor(out=h_sb[:, s], in0=act["o"][:, s], in1=act["c"][:, s], op=ALU.mult)
            nc.sync.dma_start(out=out[:, s], in_=h_sb[:, s])

        by_s, by_v = nc.scalar.copy, nc.vector.tensor_copy
        both = (0, 1)
        load_h()
        load_u("i")
        load_z()
        load_b()
        load_u("u")
        load_w2("i")
        load_w2("u")
        load_w("o",0)
        load_w("o",1)
        load_u("o")
        load_fc()
        warm_ps = sums.tile([P, CH], F32, tag="sums", name="warm_ps")

        def keep_warm():
            nc.tensor.matmul(
                out=warm_ps[:, 0:96], lhsT=warm[:], rhs=warm[:, 0:96], start=True, stop=True
            )

        for i in range(3):
            keep_warm()
        flip_h()
        copy_h()
        flip_u("i")
        keep_warm()
        copy_u("i",by_s)
        flip_w("z")
        copy_w("z",by_s)
        flip_b()
        copy_b()
        plain("i",(0,))
        flip_u("u")
        copy_u("u",by_s)
        spread_b()
        quantise("z")
        copy_bb()
        plain("i",(1,))
        add_bias("i")
        flip_w("i0")
        copy_w("i0",by_s)
        flip_w("i1")
        copy_w("i1",by_s)
        plain("u",(0,))
        quantise("i0")
        quantise("i1")
        flip_w("u0")
        copy_w("u0",by_s)
        flip_w("u1")
        copy_w("u1",by_s)
        plain("u",(1,))
        quantise("u0")
        add_bias("u")
        flip_w("o0")
        copy_w("o0",by_s)
        quantise("u1")
        flip_w("o1",(0,))
        flip_w("o1",(1,))
        copy_w("o1",by_s,(0,))
        flip_u("o")
        copy_w("o1",by_s,(1,))
        quantise("o0")
        products("i",both)
        add_mx("i",both)
        copy_u("o",by_s)
        activate("i",both)
        products("u",both)
        add_mx("u",both)
        activate("u",(0,))
        activate("u",(1,))
        products("o",(0,))
        plain("o")
        quantise("o1",(0,))
        quantise("o1",(1,))
        add_bias("o")
        products("o",(1,))
        times_iu((0,))
        times_iu((1,))
        add_mx("o",(0,))
        activate("o",(0,))
        add_fc((0,))
        activate("c",(0,))
        add_fc((1,))
        activate("c",(1,))
        store_c()
        add_mx("o",(1,))
        activate("o",(1,))
        times_o((0,))
        times_o((1,))
